import numpy as np
import ml_dtypes


def mxq(x, axis, fmt="e4m3"):
    dtype, down = {"e4m3": (ml_dtypes.float8_e4m3fn, 7), "e5m2": (ml_dtypes.float8_e5m2, 14)}[fmt]
    v = np.moveaxis(np.asarray(x, np.float32).astype(ml_dtypes.bfloat16).astype(np.float64), axis, -1)
    blocks = v.reshape(v.shape[:-1] + (-1, 32))
    amax = np.abs(blocks).max(-1, keepdims=True)
    byte = np.maximum(np.where(amax > 0, np.frexp(amax)[1] - 1 + 127, 0) - down, 1)
    scale = np.exp2(byte - 127.0)
    codes = (blocks / scale).astype(np.float32).astype(dtype).astype(np.float64)
    return np.moveaxis((codes * scale).reshape(v.shape), -1, axis)


WIDE = False


def mx_kscale(k):
    if not WIDE:
        return np.ones(k)
    levels = np.array([10, -10, 5, -5, 0])
    a = np.random.permutation(np.resize(levels, k // 512 * 4)).reshape(k // 512, 4)
    idx = np.arange(k)
    return np.exp2(a[idx // 512, idx % 128 // 32])


BF16 = ml_dtypes.bfloat16


def bf(x):
    return np.asarray(x, np.float32).astype(BF16)


def f64(x):
    return np.asarray(x).astype(np.float64)


E2M1 = np.array([0.0, 0.5, 1.0, 1.5, 2.0, 3.0, 4.0, 6.0, -0.0, -0.5, -1.0, -1.5, -2.0, -3.0, -4.0, -6.0])


def pack_weight(w, fmt):
    k, n = w.shape
    w = f64(bf(w)).reshape(k // 32, 32, n)
    amax = np.abs(w).max(1)
    if fmt == "e4m3":
        byte = np.frexp(amax)[1] - 1 + 127 - 7
    else:
        mant, ex = np.frexp(amax / 6.0)
        byte = np.where(mant > 0.5, ex, ex - 1) + 127
    byte = np.clip(np.where(amax > 0, byte, 1), 1, 254)
    scaled = (w * np.exp2(127.0 - byte)[:, None, :]).reshape(k, n).astype(np.float32)
    by_word = np.ascontiguousarray(scaled.reshape(k // 512, 128, 4, n).transpose(0, 1, 3, 2))
    if fmt == "e4m3":
        words = by_word.astype(ml_dtypes.float8_e4m3fn).view(np.uint8)
    else:
        c = by_word.astype(ml_dtypes.float4_e2m1fn).view(np.uint8) & 0xF
        words = c[..., 0::2] | (c[..., 1::2] << 4)
    return np.ascontiguousarray(words), np.ascontiguousarray(byte.astype(np.uint8).reshape(k // 512, 16, n))


def unpack_weight(words, scales, fmt):
    g, p, n, _ = words.shape
    if fmt == "e4m3":
        vals = np.ascontiguousarray(words).view(ml_dtypes.float8_e4m3fn).astype(np.float64)
    else:
        nib = np.empty((g, p, n, 4), np.uint8)
        nib[..., 0::2] = words & 0xF
        nib[..., 1::2] = words >> 4
        vals = E2M1[nib]
    vals = vals * np.repeat(np.exp2(scales.astype(np.float64) - 127.0), 8, axis=1)[..., None]
    return vals.transpose(0, 1, 3, 2).reshape(g * 512, n)


B, N, D, DO, H, HID = 2, 128, 16384, 512, 8, 2048
FMT = "e4m3"


def setup_inputs():
    s, t = mx_kscale(D), mx_kscale(D)
    adj = np.random.uniform(size=(N, N))
    adj = adj / adj.sum(-1, keepdims=True)
    h_norm = bf(np.random.standard_normal((B, N, D)) * s)
    o_attn = bf(np.random.standard_normal((B, N, D)) * 0.25 * t)
    a_gcn = bf(adj + np.random.standard_normal((N, N)) * 0.5 / np.sqrt(N))
    w_proj_words, w_proj_scales = pack_weight(np.random.standard_normal((D, DO)) * 2.0 / np.sqrt(D) / t[:, None], FMT)
    b_proj = bf(np.random.standard_normal(DO) * 0.1)
    gcn_w_words, gcn_w_scales = pack_weight(np.random.standard_normal((D, DO)) / np.sqrt(D) / s[:, None], FMT)
    gcn_m = bf(1.0 + 0.1 * np.random.standard_normal(DO))
    return {
        "h_norm": h_norm,
        "o_attn": o_attn,
        "a_gcn": a_gcn,
        "w_proj_words": w_proj_words,
        "w_proj_scales": w_proj_scales,
        "b_proj": b_proj,
        "gcn_w_words": gcn_w_words,
        "gcn_w_scales": gcn_w_scales,
        "gcn_m": gcn_m,
    }


def reference(h_norm, o_attn, a_gcn, w_proj_words, w_proj_scales, b_proj, gcn_w_words, gcn_w_scales, gcn_m):
    o = (mxq(f64(o_attn), 2, "e4m3") @ unpack_weight(w_proj_words, w_proj_scales, FMT)) + f64(b_proj)
    agg = f64(a_gcn) @ f64(h_norm)
    g = (mxq(agg, 2, "e4m3") @ unpack_weight(gcn_w_words, gcn_w_scales, FMT)) * f64(gcn_m)
    return o + g

@@ -1,0 +1,227 @@
+from contextlib import ExitStack
+
+import concourse.mybir as mybir
+from concourse.masks import make_identity
+
+F32 = mybir.dt.float32
+BF16 = mybir.dt.bfloat16
+I32 = mybir.dt.int32
+U32 = mybir.dt.uint32
+U8 = mybir.dt.uint8
+FP8X4 = mybir.dt.float8_e4m3fn_x4
+MULT = mybir.AluOpType.mult
+ADD = mybir.AluOpType.add
+
+P = 128
+SAMPLES = 2
+FEATURES = 16384
+OUT = 512
+PACK = 4
+K_PASS = P * PACK
+PASSES = FEATURES // K_PASS
+BRANCHES = 2
+QUARTER = PASSES // 4
+
+CHUNK = 4
+CHUNKS = BRANCHES * PASSES // CHUNK
+ROUND = 2
+ROUNDS = BRANCHES * PASSES // ROUND
+ROUNDS_PER_CHUNK = CHUNK // ROUND
+BLOCKS = SAMPLES * CHUNK
+
+LEAD = 2
+AHEAD = 5
+
+FLOPS = 2 * BRANCHES * SAMPLES * P * FEATURES * OUT + 2 * SAMPLES * P * P * FEATURES
+
+
+def tile_gatblock_pa_k_kernel(
+    tc, h_norm, o_attn, a_gcn, w_proj_words, w_proj_scales, b_proj, gcn_w_words, gcn_w_scales, gcn_m, out
+):
+    nc = tc.nc
+    acts_of = [h_norm, o_attn]
+    words_of = [gcn_w_words, w_proj_words]
+    scales_of = [gcn_w_scales, w_proj_scales]
+
+    with ExitStack() as ctx:
+        const = ctx.enter_context(tc.tile_pool(name="const", bufs=1))
+        raw_pool = ctx.enter_context(tc.tile_pool(name="raw", bufs=AHEAD + LEAD))
+        weight_pool = ctx.enter_context(tc.tile_pool(name="weights", bufs=AHEAD + 2))
+        sorted_pool = ctx.enter_context(tc.tile_pool(name="sorted", bufs=3))
+        grouped_pool = ctx.enter_context(tc.tile_pool(name="grouped", bufs=3))
+        code_pool = ctx.enter_context(tc.tile_pool(name="codes", bufs=4))
+        sum_pool = ctx.enter_context(tc.psum_pool(name="sums", bufs=1))
+        bank_pool = ctx.enter_context(tc.psum_pool(name="banks", bufs=6))
+        ctx.enter_context(tc.manual_schedule())
+
+        planes_of = {}
+        for branch in range(BRANCHES):
+            for quarter in range(PASSES // QUARTER):
+                planes = const.tile([P, QUARTER, OUT], U8, name="planes%d%d" % (branch, quarter), align_bytes=64)
+                nc.vector.memset(planes[:].bitcast(I32), 0)
+                planes_of[(branch, quarter)] = planes
+
+        rows = const.tile([P, 2, OUT], BF16)
+        nc.vector.memset(rows[:], 0.0)
+        ones = const.tile([P, P], BF16)
+        nc.vector.memset(ones[:], 1.0)
+        nc.scalar.dma_start(out=rows[0:1, 0, :], in_=gcn_m.unsqueeze(0))
+        nc.scalar.dma_start(out=rows[0:1, 1, :], in_=b_proj.unsqueeze(0))
+        a_nodes = const.tile([P, P], BF16)
+        nc.sync.dma_start(out=a_nodes[:], in_=a_gcn)
+
+        ident_bf16 = const.tile([P, P], BF16)
+        make_identity(nc, ident_bf16[:])
+        ident_f32 = const.tile([P, P], F32)
+        make_identity(nc, ident_f32[:])
+
+        for branch in range(BRANCHES):
+            by_row = scales_of[branch].rearrange("g q n -> q g n")
+            for quarter in range(PASSES // QUARTER):
+                for r in range(4):
+                    nc.gpsimd.dma_start(
+                        out=planes_of[(branch, quarter)][:].bitcast(F32)[r:P:32, :, :],
+                        in_=by_row[r:16:4, quarter * QUARTER : (quarter + 1) * QUARTER, :].bitcast(F32),
+                    )
+
+        raw_of = {}
+        weights_of = {}
+        sorted_of = {}
+        grouped_of = {}
+        codes_of = {}
+        sums = {}
+        partial = {}
+
+        def load_acts(chunk):
+            branch, first = divmod(chunk * CHUNK, PASSES)
+            raw = raw_pool.tile([P, SAMPLES, CHUNK * K_PASS], BF16)
+            columns = slice(first * K_PASS, (first + CHUNK) * K_PASS)
+            nc.sync.dma_start(out=raw[:], in_=acts_of[branch][:, :, columns].rearrange("b i k -> i b k"))
+            raw_of[chunk] = raw
+
+        def load_weights(chunk):
+            branch, first = divmod(chunk * CHUNK, PASSES)
+            weights = weight_pool.tile([P, CHUNK, PACK * OUT], U8, align_bytes=64)
+            nc.sync.dma_start(
+                out=weights[:].bitcast(I32),
+                in_=words_of[branch][first : first + CHUNK].rearrange("g p n t -> p g (n t)").bitcast(I32),
+            )
+            weights_of[chunk] = weights
+
+        def sort_words(chunk):
+            in_order = sorted_pool.tile([P, BLOCKS, 2, 2 * P], BF16)
+            nc.vector.tensor_copy(
+                out=in_order[:].bitcast(F32),
+                in_=raw_of[chunk][:].bitcast(F32).rearrange("i b (g p u) -> i (b g) u p", g=CHUNK, u=2),
+            )
+            sorted_of[chunk] = in_order
+
+        def copy_out(bank_number, dst, src):
+            if bank_number % 4 == 3:
+                nc.vector.tensor_copy(out=dst, in_=src)
+            else:
+                nc.scalar.copy(out=dst, in_=src)
+
+        def fill(rnd):
+            chunk, first = divmod(rnd * ROUND, CHUNK)
+            in_order = sorted_of[chunk]
+            grouped = grouped_pool.tile([P, ROUND, SAMPLES, P, PACK], BF16, align_bytes=64)
+            for step in range(ROUND):
+                if chunk < CHUNKS // BRANCHES:
+                    for b in range(SAMPLES):
+                        mixed = bank_pool.tile([P, PACK, P], F32, tag="bank")
+                        for t in range(PACK):
+                            nc.tensor.matmul(
+                                out=mixed[:, t, :],
+                                lhsT=in_order[:, b * CHUNK + first + step, t // 2, t % 2 : 2 * P : 2],
+                                rhs=a_feeds[:],
+                                start=True,
+                                stop=True,
+                            )
+                        copy_out(step * SAMPLES + b, grouped[:, step, b, :, :], mixed[:].rearrange("p t i -> p i t"))
+                else:
+                    turned = bank_pool.tile([P, SAMPLES, 2, P], F32, tag="bank")
+                    for b in range(SAMPLES):
+                        for u in range(2):
+                            nc.tensor.transpose(
+                                turned[:, b, u, :],
+                                in_order[:].bitcast(F32)[:, b * CHUNK + first + step, u, :],
+                                ident_f32[:],
+                            )
+                    copy_out(step, grouped[:, step].bitcast(F32), turned[:].rearrange("p b u i -> p b i u"))
+            grouped_of[rnd] = grouped
+
+        def quantise(rnd):
+            codes = code_pool.tile([P, ROUND, SAMPLES, P], U32, align_bytes=64)
+            act_scales = code_pool.tile([P, ROUND, SAMPLES, P], U8, align_bytes=64)
+            nc.vector.quantize_mx(
+                out=codes[:].rearrange("p g b i -> p (g b i)").bitcast(FP8X4),
+                scales=act_scales[:].rearrange("p g b i -> p (g b i)"),
+                in_=grouped_of[rnd][:].rearrange("p g b i t -> p (g b i t)"),
+            )
+            codes_of[rnd] = (codes, act_scales)
+
+        def multiply(rnd):
+            chunk, first = divmod(rnd * ROUND, CHUNK)
+            branch, first_pass = divmod(rnd * ROUND, PASSES)
+            codes, act_scales = codes_of[rnd]
+            for step in range(ROUND):
+                quarter, column = divmod(first_pass + step, QUARTER)
+                for b in range(SAMPLES):
+                    nc.tensor.matmul_mx(
+                        out=sums[b][:],
+                        lhsT=codes[:, step, b, :].bitcast(FP8X4),
+                        lhsT_scale=act_scales[:, step, b, :],
+                        rhs=weights_of[chunk][:, first + step, :].bitcast(FP8X4),
+                        rhs_scale=planes_of[(branch, quarter)][:, column, :],
+                        start=(first_pass + step == 0),
+                        stop=(first_pass + step == PASSES - 1),
+                    )
+
+        for chunk in range(LEAD):
+            load_acts(chunk)
+        for chunk in range(AHEAD):
+            load_weights(chunk)
+            load_acts(chunk + LEAD)
+
+        a_turned = bank_pool.tile([P, P], BF16, tag="bank")
+        nc.tensor.transpose(a_turned[:], a_nodes[:], ident_bf16[:])
+        a_feeds = const.tile([P, P], BF16)
+        nc.scalar.copy(out=a_feeds[:], in_=a_turned[:])
+        spread = const.tile([P, 2, OUT], F32)
+
+        sort_words(0)
+        for rnd in range(ROUNDS + 2):
+            if rnd % ROUNDS_PER_CHUNK == 0:
+                chunk = rnd // ROUNDS_PER_CHUNK
+                if chunk + 1 < CHUNKS:
+                    sort_words(chunk + 1)
+                if chunk + AHEAD < CHUNKS:
+                    load_weights(chunk + AHEAD)
+                if chunk + AHEAD + LEAD < CHUNKS:
+                    load_acts(chunk + AHEAD + LEAD)
+            if rnd == ROUNDS // BRANCHES:
+                for row in range(2):
+                    summed = bank_pool.tile([P, OUT], F32, tag="bank")
+                    nc.tensor.matmul(out=summed[:], lhsT=ones[:], rhs=rows[:, row, :], start=True, stop=True)
+                    nc.scalar.copy(out=spread[:, row, :], in_=summed[:])
+            if rnd < ROUNDS:
+                fill(rnd)
+            if 1 <= rnd <= ROUNDS:
+                quantise(rnd - 1)
+            if rnd >= 2:
+                if (rnd - 2) * ROUND % PASSES == 0:
+                    for b in range(SAMPLES):
+                        sums[b] = sum_pool.tile([P, OUT], F32, name="sum%d" % b, tag="sum%d" % b)
+                multiply(rnd - 2)
+            if rnd - 2 == ROUNDS // BRANCHES - 1:
+                for b in range(SAMPLES):
+                    partial[b] = const.tile([P, OUT], F32, name="partial%d" % b)
+                    nc.vector.tensor_tensor(out=partial[b][:], in0=sums[b][:], in1=spread[:, 0, :], op=MULT)
+                for b in range(SAMPLES):
+                    nc.vector.tensor_tensor(out=partial[b][:], in0=partial[b][:], in1=spread[:, 1, :], op=ADD)
+
+        for b in range(SAMPLES):
+            result = const.tile([P, OUT], F32, name="result%d" % b)
+            nc.vector.tensor_tensor(out=result[:], in0=sums[b][:], in1=partial[b][:], op=ADD)
+            nc.sync.dma_start(out=out[b], in_=result[:])

@@ -20,7 +20,7 @@ PACK = 4
 K_PASS = P * PACK
 PASSES = FEATURES // K_PASS
 BRANCHES = 2
-QUARTER = PASSES // 4
+GROUP = 4
 
 CHUNK = 4
 CHUNKS = BRANCHES * PASSES // CHUNK
@@ -56,10 +56,9 @@ def tile_gatblock_pa_k_kernel(
 
         planes_of = {}
         for branch in range(BRANCHES):
-            for quarter in range(PASSES // QUARTER):
-                planes = const.tile([P, QUARTER, OUT], U8, name="planes%d%d" % (branch, quarter), align_bytes=64)
-                nc.vector.memset(planes[:].bitcast(I32), 0)
-                planes_of[(branch, quarter)] = planes
+            planes = const.tile([P, PASSES // GROUP, OUT], U8, name="planes%d" % branch, align_bytes=64)
+            nc.vector.memset(planes[:].bitcast(I32), 0)
+            planes_of[branch] = planes
 
         rows = const.tile([P, 2, OUT], BF16)
         nc.vector.memset(rows[:], 0.0)
@@ -75,14 +74,14 @@ def tile_gatblock_pa_k_kernel(
         ident_f32 = const.tile([P, P], F32)
         make_identity(nc, ident_f32[:])
 
-        for branch in range(BRANCHES):
-            by_row = scales_of[branch].rearrange("g q n -> q g n")
-            for quarter in range(PASSES // QUARTER):
-                for r in range(4):
-                    nc.gpsimd.dma_start(
-                        out=planes_of[(branch, quarter)][:].bitcast(F32)[r:P:32, :, :],
-                        in_=by_row[r:16:4, quarter * QUARTER : (quarter + 1) * QUARTER, :].bitcast(F32),
-                    )
+        def load_scales(branch):
+            by_plane = scales_of[branch].rearrange("(m j) q n -> j q m n", j=GROUP)
+            for q in range(16):
+                first = 32 * (q // 4) + q % 4
+                nc.sync.dma_start(
+                    out=planes_of[branch][:].bitcast(I32)[first : first + 4 * GROUP : 4, :, :],
+                    in_=by_plane[:, q, :, :].bitcast(I32),
+                )
 
         raw_of = {}
         weights_of = {}
@@ -166,19 +165,21 @@ def tile_gatblock_pa_k_kernel(
             branch, first_pass = divmod(rnd * ROUND, PASSES)
             codes, act_scales = codes_of[rnd]
             for step in range(ROUND):
-                quarter, column = divmod(first_pass + step, QUARTER)
+                column, plane = divmod(first_pass + step, GROUP)
                 for b in range(SAMPLES):
                     nc.tensor.matmul_mx(
                         out=sums[b][:],
                         lhsT=codes[:, step, b, :].bitcast(FP8X4),
                         lhsT_scale=act_scales[:, step, b, :],
                         rhs=weights_of[chunk][:, first + step, :].bitcast(FP8X4),
-                        rhs_scale=planes_of[(branch, quarter)][:, column, :],
+                        rhs_scale=planes_of[branch][4 * plane : P, column, :],
                         start=(first_pass + step == 0),
                         stop=(first_pass + step == PASSES - 1),
                     )
 
-        for chunk in range(LEAD):
+        load_acts(0)
+        load_scales(0)
+        for chunk in range(1, LEAD):
             load_acts(chunk)
         for chunk in range(AHEAD):
             load_weights(chunk)
@@ -196,6 +197,8 @@ def tile_gatblock_pa_k_kernel(
                 chunk = rnd // ROUNDS_PER_CHUNK
                 if chunk + 1 < CHUNKS:
                     sort_words(chunk + 1)
+                if chunk + AHEAD == CHUNKS // BRANCHES:
+                    load_scales(1)
                 if chunk + AHEAD < CHUNKS:
                     load_weights(chunk + AHEAD)
                 if chunk + AHEAD + LEAD < CHUNKS:

@@ -115,15 +115,14 @@ def tile_gatblock_pa_k_kernel(
             )
             sorted_of[chunk] = in_order
 
-        def copy_out(bank_number, dst, src):
-            if bank_number % 4 == 3:
+        def copy_out(on_vector, dst, src):
+            if on_vector:
                 nc.vector.tensor_copy(out=dst, in_=src)
             else:
                 nc.scalar.copy(out=dst, in_=src)
 
         def fill(rnd):
             chunk, first = divmod(rnd * ROUND, CHUNK)
-            in_order = sorted_of[chunk]
             grouped = grouped_pool.tile([P, ROUND, SAMPLES, P, PACK], BF16, align_bytes=64)
             for step in range(ROUND):
                 if chunk < CHUNKS // BRANCHES:
@@ -132,13 +131,15 @@ def tile_gatblock_pa_k_kernel(
                         for t in range(PACK):
                             nc.tensor.matmul(
                                 out=mixed[:, t, :],
-                                lhsT=in_order[:, b * CHUNK + first + step, t // 2, t % 2 : 2 * P : 2],
+                                lhsT=raw_of[chunk][:, b, (first + step) * K_PASS + t : (first + step + 1) * K_PASS : PACK],
                                 rhs=a_feeds[:],
                                 start=True,
                                 stop=True,
                             )
-                        copy_out(step * SAMPLES + b, grouped[:, step, b, :, :], mixed[:].rearrange("p t i -> p i t"))
+                        bank_number = (rnd * ROUND + step) * SAMPLES + b
+                        copy_out(bank_number % 8 in (1, 3, 6), grouped[:, step, b, :, :], mixed[:].rearrange("p t i -> p i t"))
                 else:
+                    in_order = sorted_of[chunk]
                     turned = bank_pool.tile([P, SAMPLES, 2, P], F32, tag="bank")
                     for b in range(SAMPLES):
                         for u in range(2):
@@ -147,7 +148,7 @@ def tile_gatblock_pa_k_kernel(
                                 in_order[:].bitcast(F32)[:, b * CHUNK + first + step, u, :],
                                 ident_f32[:],
                             )
-                    copy_out(step, grouped[:, step].bitcast(F32), turned[:].rearrange("p b u i -> p b i u"))
+                    copy_out(False, grouped[:, step].bitcast(F32), turned[:].rearrange("p b u i -> p b i u"))
             grouped_of[rnd] = grouped
 
         def quantise(rnd):
@@ -191,11 +192,10 @@ def tile_gatblock_pa_k_kernel(
         nc.scalar.copy(out=a_feeds[:], in_=a_turned[:])
         spread = const.tile([P, 2, OUT], F32)
 
-        sort_words(0)
         for rnd in range(ROUNDS + 2):
             if rnd % ROUNDS_PER_CHUNK == 0:
                 chunk = rnd // ROUNDS_PER_CHUNK
-                if chunk + 1 < CHUNKS:
+                if CHUNKS // BRANCHES <= chunk + 1 < CHUNKS:
                     sort_words(chunk + 1)
                 if chunk + AHEAD == CHUNKS // BRANCHES:
                     load_scales(1)

@@ -101,10 +101,12 @@ def tile_gatblock_pa_k_kernel(
         def load_weights(chunk):
             branch, first = divmod(chunk * CHUNK, PASSES)
             weights = weight_pool.tile([P, CHUNK, PACK * OUT], U8, align_bytes=64)
-            nc.sync.dma_start(
-                out=weights[:].bitcast(I32),
-                in_=words_of[branch][first : first + CHUNK].rearrange("g p n t -> p g (n t)").bitcast(I32),
-            )
+            step = 1 if chunk == CHUNKS - 1 else CHUNK
+            for g in range(0, CHUNK, step):
+                nc.sync.dma_start(
+                    out=weights[:, g : g + step, :].bitcast(I32),
+                    in_=words_of[branch][first + g : first + g + step].rearrange("g p n t -> p g (n t)").bitcast(I32),
+                )
             weights_of[chunk] = weights
 
         def sort_words(chunk):
@@ -180,6 +182,7 @@ def tile_gatblock_pa_k_kernel(
 
         load_acts(0)
         load_scales(0)
+        load_scales(1)
         for chunk in range(1, LEAD):
             load_acts(chunk)
         for chunk in range(AHEAD):
@@ -197,8 +200,6 @@ def tile_gatblock_pa_k_kernel(
                 chunk = rnd // ROUNDS_PER_CHUNK
                 if CHUNKS // BRANCHES <= chunk + 1 < CHUNKS:
                     sort_words(chunk + 1)
-                if chunk + AHEAD == CHUNKS // BRANCHES:
-                    load_scales(1)
                 if chunk + AHEAD < CHUNKS:
                     load_weights(chunk + AHEAD)
                 if chunk + AHEAD + LEAD < CHUNKS:

@@ -209,8 +209,11 @@ def tile_gatblock_pa_k_kernel(
                     summed = bank_pool.tile([P, OUT], F32, tag="bank")
                     nc.tensor.matmul(out=summed[:], lhsT=ones[:], rhs=rows[:, row, :], start=True, stop=True)
                     nc.scalar.copy(out=spread[:, row, :], in_=summed[:])
-            if rnd < ROUNDS:
+            if rnd < ROUNDS // BRANCHES:
                 fill(rnd)
+            elif rnd < ROUNDS and rnd % 2 == 0:
+                fill(rnd)
+                fill(rnd + 1)
             if 1 <= rnd <= ROUNDS:
                 quantise(rnd - 1)
             if rnd >= 2:

@@ -76,11 +76,12 @@ def tile_gatblock_pa_k_kernel(
 
         def load_scales(branch):
             by_plane = scales_of[branch].rearrange("(m j) q n -> j q m n", j=GROUP)
+            queue, words = (nc.sync, I32) if branch == 0 else (nc.gpsimd, F32)
             for q in range(16):
                 first = 32 * (q // 4) + q % 4
-                nc.sync.dma_start(
-                    out=planes_of[branch][:].bitcast(I32)[first : first + 4 * GROUP : 4, :, :],
-                    in_=by_plane[:, q, :, :].bitcast(I32),
+                queue.dma_start(
+                    out=planes_of[branch][:].bitcast(words)[first : first + 4 * GROUP : 4, :, :],
+                    in_=by_plane[:, q, :, :].bitcast(words),
                 )
 
         raw_of = {}

from contextlib import ExitStack

import concourse.mybir as mybir
from concourse.masks import make_identity

F32 = mybir.dt.float32
BF16 = mybir.dt.bfloat16
I32 = mybir.dt.int32
U32 = mybir.dt.uint32
U8 = mybir.dt.uint8
FP8X4 = mybir.dt.float8_e4m3fn_x4
MULT = mybir.AluOpType.mult
ADD = mybir.AluOpType.add

P = 128
SAMPLES = 2
FEATURES = 16384
OUT = 512
PACK = 4
K_PASS = P * PACK
PASSES = FEATURES // K_PASS
BRANCHES = 2
GROUP = 4

CHUNK = 4
CHUNKS = BRANCHES * PASSES // CHUNK
ROUND = 2
ROUNDS = BRANCHES * PASSES // ROUND
ROUNDS_PER_CHUNK = CHUNK // ROUND
BLOCKS = SAMPLES * CHUNK

LEAD = 2
AHEAD = 5

FLOPS = 2 * BRANCHES * SAMPLES * P * FEATURES * OUT + 2 * SAMPLES * P * P * FEATURES


def tile_gatblock_pa_k_kernel(
    tc, h_norm, o_attn, a_gcn, w_proj_words, w_proj_scales, b_proj, gcn_w_words, gcn_w_scales, gcn_m, out
):
    nc = tc.nc
    acts_of = [h_norm, o_attn]
    words_of = [gcn_w_words, w_proj_words]
    scales_of = [gcn_w_scales, w_proj_scales]

    with ExitStack() as ctx:
        const = ctx.enter_context(tc.tile_pool(name="const", bufs=1))
        raw_pool = ctx.enter_context(tc.tile_pool(name="raw", bufs=AHEAD + LEAD))
        weight_pool = ctx.enter_context(tc.tile_pool(name="weights", bufs=AHEAD + 2))
        sorted_pool = ctx.enter_context(tc.tile_pool(name="sorted", bufs=3))
        grouped_pool = ctx.enter_context(tc.tile_pool(name="grouped", bufs=3))
        code_pool = ctx.enter_context(tc.tile_pool(name="codes", bufs=4))
        sum_pool = ctx.enter_context(tc.psum_pool(name="sums", bufs=1))
        bank_pool = ctx.enter_context(tc.psum_pool(name="banks", bufs=6))
        ctx.enter_context(tc.manual_schedule())

        planes_of = {}
        for branch in range(BRANCHES):
            planes = const.tile([P, PASSES // GROUP, OUT], U8, name="planes%d" % branch, align_bytes=64)
            nc.vector.memset(planes[:].bitcast(I32), 0)
            planes_of[branch] = planes

        rows = const.tile([P, 2, OUT], BF16)
        nc.vector.memset(rows[:], 0.0)
        ones = const.tile([P, P], BF16)
        nc.vector.memset(ones[:], 1.0)
        nc.scalar.dma_start(out=rows[0:1, 0, :], in_=gcn_m.unsqueeze(0))
        nc.scalar.dma_start(out=rows[0:1, 1, :], in_=b_proj.unsqueeze(0))
        a_nodes = const.tile([P, P], BF16)
        nc.sync.dma_start(out=a_nodes[:], in_=a_gcn)

        ident_bf16 = const.tile([P, P], BF16)
        make_identity(nc, ident_bf16[:])
        ident_f32 = const.tile([P, P], F32)
        make_identity(nc, ident_f32[:])

        def load_scales(branch):
            by_plane = scales_of[branch].rearrange("(m j) q n -> j q m n", j=GROUP)
            queue, words = (nc.sync, I32) if branch == 0 else (nc.gpsimd, F32)
            for q in range(16):
                first = 32 * (q // 4) + q % 4
                queue.dma_start(
                    out=planes_of[branch][:].bitcast(words)[first : first + 4 * GROUP : 4, :, :],
                    in_=by_plane[:, q, :, :].bitcast(words),
                )

        raw_of = {}
        weights_of = {}
        sorted_of = {}
        grouped_of = {}
        codes_of = {}
        sums = {}
        partial = {}

        def load_acts(chunk):
            branch, first = divmod(chunk * CHUNK, PASSES)
            raw = raw_pool.tile([P, SAMPLES, CHUNK * K_PASS], BF16)
            columns = slice(first * K_PASS, (first + CHUNK) * K_PASS)
            nc.sync.dma_start(out=raw[:], in_=acts_of[branch][:, :, columns].rearrange("b i k -> i b k"))
            raw_of[chunk] = raw

        def load_weights(chunk):
            branch, first = divmod(chunk * CHUNK, PASSES)
            weights = weight_pool.tile([P, CHUNK, PACK * OUT], U8, align_bytes=64)
            step = 1 if chunk == CHUNKS - 1 else CHUNK
            for g in range(0, CHUNK, step):
                nc.sync.dma_start(
                    out=weights[:, g : g + step, :].bitcast(I32),
                    in_=words_of[branch][first + g : first + g + step].rearrange("g p n t -> p g (n t)").bitcast(I32),
                )
            weights_of[chunk] = weights

        def sort_words(chunk):
            in_order = sorted_pool.tile([P, BLOCKS, 2, 2 * P], BF16)
            nc.vector.tensor_copy(
                out=in_order[:].bitcast(F32),
                in_=raw_of[chunk][:].bitcast(F32).rearrange("i b (g p u) -> i (b g) u p", g=CHUNK, u=2),
            )
            sorted_of[chunk] = in_order

        def copy_out(on_vector, dst, src):
            if on_vector:
                nc.vector.tensor_copy(out=dst, in_=src)
            else:
                nc.scalar.copy(out=dst, in_=src)

        def fill(rnd):
            chunk, first = divmod(rnd * ROUND, CHUNK)
            grouped = grouped_pool.tile([P, ROUND, SAMPLES, P, PACK], BF16, align_bytes=64)
            for step in range(ROUND):
                if chunk < CHUNKS // BRANCHES:
                    for b in range(SAMPLES):
                        mixed = bank_pool.tile([P, PACK, P], F32, tag="bank")
                        for t in range(PACK):
                            nc.tensor.matmul(
                                out=mixed[:, t, :],
                                lhsT=raw_of[chunk][:, b, (first + step) * K_PASS + t : (first + step + 1) * K_PASS : PACK],
                                rhs=a_feeds[:],
                                start=True,
                                stop=True,
                            )
                        bank_number = (rnd * ROUND + step) * SAMPLES + b
                        copy_out(bank_number % 8 in (1, 3, 6), grouped[:, step, b, :, :], mixed[:].rearrange("p t i -> p i t"))
                else:
                    in_order = sorted_of[chunk]
                    turned = bank_pool.tile([P, SAMPLES, 2, P], F32, tag="bank")
                    for b in range(SAMPLES):
                        for u in range(2):
                            nc.tensor.transpose(
                                turned[:, b, u, :],
                                in_order[:].bitcast(F32)[:, b * CHUNK + first + step, u, :],
                                ident_f32[:],
                            )
                    copy_out(False, grouped[:, step].bitcast(F32), turned[:].rearrange("p b u i -> p b i u"))
            grouped_of[rnd] = grouped

        def quantise(rnd):
            codes = code_pool.tile([P, ROUND, SAMPLES, P], U32, align_bytes=64)
            act_scales = code_pool.tile([P, ROUND, SAMPLES, P], U8, align_bytes=64)
            nc.vector.quantize_mx(
                out=codes[:].rearrange("p g b i -> p (g b i)").bitcast(FP8X4),
                scales=act_scales[:].rearrange("p g b i -> p (g b i)"),
                in_=grouped_of[rnd][:].rearrange("p g b i t -> p (g b i t)"),
            )
            codes_of[rnd] = (codes, act_scales)

        def multiply(rnd):
            chunk, first = divmod(rnd * ROUND, CHUNK)
            branch, first_pass = divmod(rnd * ROUND, PASSES)
            codes, act_scales = codes_of[rnd]
            for step in range(ROUND):
                column, plane = divmod(first_pass + step, GROUP)
                for b in range(SAMPLES):
                    nc.tensor.matmul_mx(
                        out=sums[b][:],
                        lhsT=codes[:, step, b, :].bitcast(FP8X4),
                        lhsT_scale=act_scales[:, step, b, :],
                        rhs=weights_of[chunk][:, first + step, :].bitcast(FP8X4),
                        rhs_scale=planes_of[branch][4 * plane : P, column, :],
                        start=(first_pass + step == 0),
                        stop=(first_pass + step == PASSES - 1),
                    )

        load_acts(0)
        load_scales(0)
        load_scales(1)
        for chunk in range(1, LEAD):
            load_acts(chunk)
        for chunk in range(AHEAD):
            load_weights(chunk)
            load_acts(chunk + LEAD)

        a_turned = bank_pool.tile([P, P], BF16, tag="bank")
        nc.tensor.transpose(a_turned[:], a_nodes[:], ident_bf16[:])
        a_feeds = const.tile([P, P], BF16)
        nc.scalar.copy(out=a_feeds[:], in_=a_turned[:])
        spread = const.tile([P, 2, OUT], F32)

        for rnd in range(ROUNDS + 2):
            if rnd % ROUNDS_PER_CHUNK == 0:
                chunk = rnd // ROUNDS_PER_CHUNK
                if CHUNKS // BRANCHES <= chunk + 1 < CHUNKS:
                    sort_words(chunk + 1)
                if chunk + AHEAD < CHUNKS:
                    load_weights(chunk + AHEAD)
                if chunk + AHEAD + LEAD < CHUNKS:
                    load_acts(chunk + AHEAD + LEAD)
            if rnd == ROUNDS // BRANCHES:
                for row in range(2):
                    summed = bank_pool.tile([P, OUT], F32, tag="bank")
                    nc.tensor.matmul(out=summed[:], lhsT=ones[:], rhs=rows[:, row, :], start=True, stop=True)
                    nc.scalar.copy(out=spread[:, row, :], in_=summed[:])
            if rnd < ROUNDS // BRANCHES:
                fill(rnd)
            elif rnd < ROUNDS and rnd % 2 == 0:
                fill(rnd)
                fill(rnd + 1)
            if 1 <= rnd <= ROUNDS:
                quantise(rnd - 1)
            if rnd >= 2:
                if (rnd - 2) * ROUND % PASSES == 0:
                    for b in range(SAMPLES):
                        sums[b] = sum_pool.tile([P, OUT], F32, name="sum%d" % b, tag="sum%d" % b)
                multiply(rnd - 2)
            if rnd - 2 == ROUNDS // BRANCHES - 1:
                for b in range(SAMPLES):
                    partial[b] = const.tile([P, OUT], F32, name="partial%d" % b)
                    nc.vector.tensor_tensor(out=partial[b][:], in0=sums[b][:], in1=spread[:, 0, :], op=MULT)
                for b in range(SAMPLES):
                    nc.vector.tensor_tensor(out=partial[b][:], in0=partial[b][:], in1=spread[:, 1, :], op=ADD)

        for b in range(SAMPLES):
            result = const.tile([P, OUT], F32, name="result%d" % b)
            nc.vector.tensor_tensor(out=result[:], in0=sums[b][:], in1=partial[b][:], op=ADD)
            nc.sync.dma_start(out=out[b], in_=result[:])
